import numpy as np
import ml_dtypes

BF16 = ml_dtypes.bfloat16


def bf(x):
    return np.asarray(x, np.float32).astype(BF16)


def f32(x):
    return np.asarray(x, np.float32)


def f64(x):
    return np.asarray(x).astype(np.float64)


def striped(idx):
    return np.tile(idx.reshape(-1, 16).T, (8, 1))


C, S, K, H, N = 512, 1024, 4, 512, 2048


def setup_inputs():
    idx = np.concatenate([np.random.permutation(S)[:H] for _ in range(K)])
    return {"tok_emb": f32(np.random.standard_normal((C, S))), "dp_pos": f32(np.random.standard_normal((C, K))), "sp_pos": f32(np.random.standard_normal((C, H))), "offs": striped(idx)}


def reference(tok_emb, dp_pos, sp_pos, offs):
    idx = offs[:16].T.reshape(-1)
    tokens = f64(tok_emb)[:, idx] + np.repeat(f64(dp_pos), H, axis=1)
    spatial = tokens.reshape(C, K, H).sum(axis=1) + f64(sp_pos)
    return np.concatenate([tokens, spatial], axis=1)

@@ -1,0 +1,59 @@
+import concourse.mybir as mybir
+
+F32 = mybir.dt.float32
+U16 = mybir.dt.uint16
+ADD = mybir.AluOpType.add
+COPY = mybir.ActivationFunctionType.Copy
+
+P = 128
+FEATURES = 512
+CODES = 1024
+DEPTHS = 4
+PLACES = 512
+ENTRIES = DEPTHS * PLACES
+BLOCKS = FEATURES // P
+
+
+def tile_rqtransformer_kernel(tc, tok_emb, dp_pos, sp_pos, offs, out):
+    nc = tc.nc
+    with tc.tile_pool(name="held", bufs=1) as held:
+        offsets = held.tile([P, ENTRIES // 16], U16, name="offsets")
+        nc.sync.dma_start(offsets[:], offs)
+
+        depth_pos = held.tile([P, BLOCKS, DEPTHS], F32, name="depth_pos")
+        nc.scalar.dma_start(depth_pos[:], dp_pos.rearrange("(b p) k -> p b k", p=P))
+
+        tables, place_pos = [], []
+        for b in range(BLOCKS):
+            rows = slice(b * P, (b + 1) * P)
+            tables.append(held.tile([P, CODES], F32, name=f"table{b}"))
+            nc.sync.dma_start(tables[b][:], tok_emb[rows, :])
+            place_pos.append(held.tile([P, PLACES], F32, name=f"place_pos{b}"))
+            nc.sync.dma_start(place_pos[b][:], sp_pos[rows, :])
+
+        depth_rows = []
+        for b in range(BLOCKS):
+            depth_rows.append(held.tile([P, ENTRIES], F32, name=f"depth_rows{b}"))
+            for k in range(DEPTHS):
+                nc.scalar.activation(
+                    depth_rows[b][:, k * PLACES : (k + 1) * PLACES],
+                    depth_pos[:, b, k : k + 1].to_broadcast([P, PLACES]),
+                    COPY,
+                )
+
+        for b in range(BLOCKS):
+            rows = slice(b * P, (b + 1) * P)
+            result = held.tile([P, ENTRIES + PLACES], F32, name=f"result{b}")
+            total = result[:, ENTRIES:]
+            for k in range(DEPTHS):
+                columns = slice(k * PLACES, (k + 1) * PLACES)
+                tokens = result[:, columns]
+                nc.vector.tensor_tensor(
+                    tokens,
+                    tables[b][:].indirect(offsets[:, k * (PLACES // 16) : (k + 1) * (PLACES // 16)]),
+                    depth_rows[b][:, columns],
+                    ADD,
+                )
+                nc.sync.dma_start(out[rows, columns], tokens)
+                nc.vector.tensor_tensor(total, place_pos[b][:] if k == 0 else total, tokens, ADD)
+            nc.sync.dma_start(out[rows, ENTRIES:], total)

@@ -1,4 +1,5 @@
 import concourse.mybir as mybir
+from concourse.masks import make_identity
 
 F32 = mybir.dt.float32
 U16 = mybir.dt.uint16
@@ -16,7 +17,7 @@ BLOCKS = FEATURES // P
 
 def tile_rqtransformer_kernel(tc, tok_emb, dp_pos, sp_pos, offs, out):
     nc = tc.nc
-    with tc.tile_pool(name="held", bufs=1) as held:
+    with tc.tile_pool(name="held", bufs=1) as held, tc.psum_pool(name="banks", bufs=1) as banks:
         offsets = held.tile([P, ENTRIES // 16], U16, name="offsets")
         nc.sync.dma_start(offsets[:], offs)
 
@@ -31,6 +32,9 @@ def tile_rqtransformer_kernel(tc, tok_emb, dp_pos, sp_pos, offs, out):
             place_pos.append(held.tile([P, PLACES], F32, name=f"place_pos{b}"))
             nc.sync.dma_start(place_pos[b][:], sp_pos[rows, :])
 
+        identity = held.tile([P, P], F32, name="identity")
+        make_identity(nc, identity[:])
+
         depth_rows = []
         for b in range(BLOCKS):
             depth_rows.append(held.tile([P, ENTRIES], F32, name=f"depth_rows{b}"))
@@ -44,7 +48,8 @@ def tile_rqtransformer_kernel(tc, tok_emb, dp_pos, sp_pos, offs, out):
         for b in range(BLOCKS):
             rows = slice(b * P, (b + 1) * P)
             result = held.tile([P, ENTRIES + PLACES], F32, name=f"result{b}")
-            total = result[:, ENTRIES:]
+            partial = banks.tile([P, PLACES], F32, name=f"partial{b}")
+            nc.tensor.matmul(partial[:], identity[:], place_pos[b][:], start=True, stop=False)
             for k in range(DEPTHS):
                 columns = slice(k * PLACES, (k + 1) * PLACES)
                 tokens = result[:, columns]
@@ -55,5 +60,8 @@ def tile_rqtransformer_kernel(tc, tok_emb, dp_pos, sp_pos, offs, out):
                     ADD,
                 )
                 nc.sync.dma_start(out[rows, columns], tokens)
-                nc.vector.tensor_tensor(total, place_pos[b][:] if k == 0 else total, tokens, ADD)
+                if k < DEPTHS - 1:
+                    nc.tensor.matmul(partial[:], identity[:], tokens, start=False, stop=(k == DEPTHS - 2))
+            total = result[:, ENTRIES:]
+            nc.vector.tensor_tensor(total, partial[:], tokens, ADD)
             nc.sync.dma_start(out[rows, ENTRIES:], total)

@@ -17,7 +17,11 @@ BLOCKS = FEATURES // P
 
 def tile_rqtransformer_kernel(tc, tok_emb, dp_pos, sp_pos, offs, out):
     nc = tc.nc
-    with tc.tile_pool(name="held", bufs=1) as held, tc.psum_pool(name="banks", bufs=1) as banks:
+    with (
+        tc.tile_pool(name="held", bufs=1) as held,
+        tc.tile_pool(name="ring", bufs=DEPTHS) as ring,
+        tc.psum_pool(name="banks", bufs=1) as banks,
+    ):
         offsets = held.tile([P, ENTRIES // 16], U16, name="offsets")
         nc.sync.dma_start(offsets[:], offs)
 
@@ -35,15 +39,7 @@ def tile_rqtransformer_kernel(tc, tok_emb, dp_pos, sp_pos, offs, out):
         identity = held.tile([P, P], F32, name="identity")
         make_identity(nc, identity[:])
 
-        depth_rows = []
-        for b in range(BLOCKS):
-            depth_rows.append(held.tile([P, ENTRIES], F32, name=f"depth_rows{b}"))
-            for k in range(DEPTHS):
-                nc.scalar.activation(
-                    depth_rows[b][:, k * PLACES : (k + 1) * PLACES],
-                    depth_pos[:, b, k : k + 1].to_broadcast([P, PLACES]),
-                    COPY,
-                )
+        store_queues = (nc.sync, nc.scalar)
 
         for b in range(BLOCKS):
             rows = slice(b * P, (b + 1) * P)
@@ -53,15 +49,17 @@ def tile_rqtransformer_kernel(tc, tok_emb, dp_pos, sp_pos, offs, out):
             for k in range(DEPTHS):
                 columns = slice(k * PLACES, (k + 1) * PLACES)
                 tokens = result[:, columns]
+                depth_row = ring.tile([P, PLACES], F32, name="depth_row")
+                nc.scalar.activation(depth_row[:], depth_pos[:, b, k : k + 1].to_broadcast([P, PLACES]), COPY)
                 nc.vector.tensor_tensor(
                     tokens,
                     tables[b][:].indirect(offsets[:, k * (PLACES // 16) : (k + 1) * (PLACES // 16)]),
-                    depth_rows[b][:, columns],
+                    depth_row[:],
                     ADD,
                 )
-                nc.sync.dma_start(out[rows, columns], tokens)
+                store_queues[(b + k) % 2].dma_start(out[rows, columns], tokens)
                 if k < DEPTHS - 1:
                     nc.tensor.matmul(partial[:], identity[:], tokens, start=False, stop=(k == DEPTHS - 2))
             total = result[:, ENTRIES:]
             nc.vector.tensor_tensor(total, partial[:], tokens, ADD)
-            nc.sync.dma_start(out[rows, ENTRIES:], total)
+            store_queues[(b + DEPTHS) % 2].dma_start(out[rows, ENTRIES:], total)

@@ -12,6 +12,7 @@ CODES = 1024
 DEPTHS = 4
 PLACES = 512
 ENTRIES = DEPTHS * PLACES
+PAIR = 2
 BLOCKS = FEATURES // P
 
 
@@ -19,7 +20,7 @@ def tile_rqtransformer_kernel(tc, tok_emb, dp_pos, sp_pos, offs, out):
     nc = tc.nc
     with (
         tc.tile_pool(name="held", bufs=1) as held,
-        tc.tile_pool(name="ring", bufs=DEPTHS) as ring,
+        tc.tile_pool(name="ring", bufs=4) as ring,
         tc.psum_pool(name="banks", bufs=1) as banks,
     ):
         offsets = held.tile([P, ENTRIES // 16], U16, name="offsets")
@@ -46,20 +47,24 @@ def tile_rqtransformer_kernel(tc, tok_emb, dp_pos, sp_pos, offs, out):
             result = held.tile([P, ENTRIES + PLACES], F32, name=f"result{b}")
             partial = banks.tile([P, PLACES], F32, name=f"partial{b}")
             nc.tensor.matmul(partial[:], identity[:], place_pos[b][:], start=True, stop=False)
-            for k in range(DEPTHS):
-                columns = slice(k * PLACES, (k + 1) * PLACES)
-                tokens = result[:, columns]
-                depth_row = ring.tile([P, PLACES], F32, name="depth_row")
-                nc.scalar.activation(depth_row[:], depth_pos[:, b, k : k + 1].to_broadcast([P, PLACES]), COPY)
+            for first in range(0, DEPTHS, PAIR):
+                columns = slice(first * PLACES, (first + PAIR) * PLACES)
+                depth_rows = ring.tile([P, PAIR * PLACES], F32, name="depth_rows")
+                nc.scalar.activation(
+                    depth_rows[:].rearrange("p (i t) -> p i t", i=PAIR),
+                    depth_pos[:, b, first : first + PAIR].unsqueeze(2).to_broadcast([P, PAIR, PLACES]),
+                    COPY,
+                )
                 nc.vector.tensor_tensor(
-                    tokens,
-                    tables[b][:].indirect(offsets[:, k * (PLACES // 16) : (k + 1) * (PLACES // 16)]),
-                    depth_row[:],
+                    result[:, columns],
+                    tables[b][:].indirect(offsets[:, first * (PLACES // 16) : (first + PAIR) * (PLACES // 16)]),
+                    depth_rows[:],
                     ADD,
                 )
-                store_queues[(b + k) % 2].dma_start(out[rows, columns], tokens)
-                if k < DEPTHS - 1:
+                store_queues[(b + first // PAIR) % 2].dma_start(out[rows, columns], result[:, columns])
+                for k in range(first, min(first + PAIR, DEPTHS - 1)):
+                    tokens = result[:, k * PLACES : (k + 1) * PLACES]
                     nc.tensor.matmul(partial[:], identity[:], tokens, start=False, stop=(k == DEPTHS - 2))
             total = result[:, ENTRIES:]
-            nc.vector.tensor_tensor(total, partial[:], tokens, ADD)
-            store_queues[(b + DEPTHS) % 2].dma_start(out[rows, ENTRIES:], total)
+            nc.vector.tensor_tensor(total, partial[:], result[:, ENTRIES - PLACES : ENTRIES], ADD)
+            store_queues[b % 2].dma_start(out[rows, ENTRIES:], total)

@@ -14,6 +14,7 @@ PLACES = 512
 ENTRIES = DEPTHS * PLACES
 PAIR = 2
 BLOCKS = FEATURES // P
+TURNS = 2
 
 
 def tile_rqtransformer_kernel(tc, tok_emb, dp_pos, sp_pos, offs, out):
@@ -42,29 +43,41 @@ def tile_rqtransformer_kernel(tc, tok_emb, dp_pos, sp_pos, offs, out):
 
         store_queues = (nc.sync, nc.scalar)
 
+        results, partials = [], []
         for b in range(BLOCKS):
-            rows = slice(b * P, (b + 1) * P)
-            result = held.tile([P, ENTRIES + PLACES], F32, name=f"result{b}")
-            partial = banks.tile([P, PLACES], F32, name=f"partial{b}")
-            nc.tensor.matmul(partial[:], identity[:], place_pos[b][:], start=True, stop=False)
+            results.append(held.tile([P, ENTRIES + PLACES], F32, name=f"result{b}"))
+            partials.append(banks.tile([P, PLACES], F32, name=f"partial{b}"))
+            nc.tensor.matmul(partials[b][:], identity[:], place_pos[b][:], start=True, stop=False)
+
+        def gather_pair(b, first):
+            columns = slice(first * PLACES, (first + PAIR) * PLACES)
+            depth_rows = ring.tile([P, PAIR * PLACES], F32, name="depth_rows")
+            spread_out = depth_rows[:].rearrange("p (i t) -> p i t", i=PAIR)
+            spread_in = depth_pos[:, b, first : first + PAIR].unsqueeze(2).to_broadcast([P, PAIR, PLACES])
+            if b == 0 and first == 0:
+                nc.vector.tensor_copy(spread_out, spread_in)
+            else:
+                nc.scalar.activation(spread_out, spread_in, COPY)
+            nc.vector.tensor_tensor(
+                results[b][:, columns],
+                tables[b][:].indirect(offsets[:, first * (PLACES // 16) : (first + PAIR) * (PLACES // 16)]),
+                depth_rows[:],
+                ADD,
+            )
+            store_queues[(b + first // PAIR) % 2].dma_start(out[b * P : (b + 1) * P, columns], results[b][:, columns])
+            for k in range(first, min(first + PAIR, DEPTHS - 1)):
+                tokens = results[b][:, k * PLACES : (k + 1) * PLACES]
+                nc.tensor.matmul(partials[b][:], identity[:], tokens, start=False, stop=(k == DEPTHS - 2))
+
+        def finish(b):
+            total = results[b][:, ENTRIES:]
+            nc.vector.tensor_tensor(total, partials[b][:], results[b][:, ENTRIES - PLACES : ENTRIES], ADD)
+            nc.sync.dma_start(out[b * P : (b + 1) * P, ENTRIES:], total)
+
+        for group in range(0, BLOCKS, TURNS):
+            blocks = range(group, group + TURNS)
             for first in range(0, DEPTHS, PAIR):
-                columns = slice(first * PLACES, (first + PAIR) * PLACES)
-                depth_rows = ring.tile([P, PAIR * PLACES], F32, name="depth_rows")
-                nc.scalar.activation(
-                    depth_rows[:].rearrange("p (i t) -> p i t", i=PAIR),
-                    depth_pos[:, b, first : first + PAIR].unsqueeze(2).to_broadcast([P, PAIR, PLACES]),
-                    COPY,
-                )
-                nc.vector.tensor_tensor(
-                    result[:, columns],
-                    tables[b][:].indirect(offsets[:, first * (PLACES // 16) : (first + PAIR) * (PLACES // 16)]),
-                    depth_rows[:],
-                    ADD,
-                )
-                store_queues[(b + first // PAIR) % 2].dma_start(out[rows, columns], result[:, columns])
-                for k in range(first, min(first + PAIR, DEPTHS - 1)):
-                    tokens = result[:, k * PLACES : (k + 1) * PLACES]
-                    nc.tensor.matmul(partial[:], identity[:], tokens, start=False, stop=(k == DEPTHS - 2))
-            total = result[:, ENTRIES:]
-            nc.vector.tensor_tensor(total, partial[:], result[:, ENTRIES - PLACES : ENTRIES], ADD)
-            store_queues[b % 2].dma_start(out[rows, ENTRIES:], total)
+                for b in blocks:
+                    gather_pair(b, first)
+            for b in blocks:
+                finish(b)

@@ -27,16 +27,19 @@ def tile_rqtransformer_kernel(tc, tok_emb, dp_pos, sp_pos, offs, out):
         offsets = held.tile([P, ENTRIES // 16], U16, name="offsets")
         nc.sync.dma_start(offsets[:], offs)
 
+        table_blocks = tok_emb.rearrange("(p b) v -> b p v", b=BLOCKS)
+        place_blocks = sp_pos.rearrange("(p b) t -> b p t", b=BLOCKS)
+        out_blocks = out.rearrange("(p b) j -> b p j", b=BLOCKS)
+
         depth_pos = held.tile([P, BLOCKS, DEPTHS], F32, name="depth_pos")
-        nc.scalar.dma_start(depth_pos[:], dp_pos.rearrange("(b p) k -> p b k", p=P))
+        nc.scalar.dma_start(depth_pos[:], dp_pos.rearrange("(p b) k -> p b k", b=BLOCKS))
 
         tables, place_pos = [], []
         for b in range(BLOCKS):
-            rows = slice(b * P, (b + 1) * P)
             tables.append(held.tile([P, CODES], F32, name=f"table{b}"))
-            nc.sync.dma_start(tables[b][:], tok_emb[rows, :])
+            nc.sync.dma_start(tables[b][:], table_blocks[b])
             place_pos.append(held.tile([P, PLACES], F32, name=f"place_pos{b}"))
-            nc.sync.dma_start(place_pos[b][:], sp_pos[rows, :])
+            nc.sync.dma_start(place_pos[b][:], place_blocks[b])
 
         identity = held.tile([P, P], F32, name="identity")
         make_identity(nc, identity[:])
@@ -64,7 +67,7 @@ def tile_rqtransformer_kernel(tc, tok_emb, dp_pos, sp_pos, offs, out):
                 depth_rows[:],
                 ADD,
             )
-            store_queues[(b + first // PAIR) % 2].dma_start(out[b * P : (b + 1) * P, columns], results[b][:, columns])
+            store_queues[(b + first // PAIR) % 2].dma_start(out_blocks[b][:, columns], results[b][:, columns])
             for k in range(first, min(first + PAIR, DEPTHS - 1)):
                 tokens = results[b][:, k * PLACES : (k + 1) * PLACES]
                 nc.tensor.matmul(partials[b][:], identity[:], tokens, start=False, stop=(k == DEPTHS - 2))
@@ -72,7 +75,7 @@ def tile_rqtransformer_kernel(tc, tok_emb, dp_pos, sp_pos, offs, out):
         def finish(b):
             total = results[b][:, ENTRIES:]
             nc.vector.tensor_tensor(total, partials[b][:], results[b][:, ENTRIES - PLACES : ENTRIES], ADD)
-            nc.sync.dma_start(out[b * P : (b + 1) * P, ENTRIES:], total)
+            nc.sync.dma_start(out_blocks[b][:, ENTRIES:], total)
 
         for group in range(0, BLOCKS, TURNS):
             blocks = range(group, group + TURNS)

@@ -52,23 +52,23 @@ def tile_rqtransformer_kernel(tc, tok_emb, dp_pos, sp_pos, offs, out):
             partials.append(banks.tile([P, PLACES], F32, name=f"partial{b}"))
             nc.tensor.matmul(partials[b][:], identity[:], place_pos[b][:], start=True, stop=False)
 
-        def gather_pair(b, first):
-            columns = slice(first * PLACES, (first + PAIR) * PLACES)
-            depth_rows = ring.tile([P, PAIR * PLACES], F32, name="depth_rows")
-            spread_out = depth_rows[:].rearrange("p (i t) -> p i t", i=PAIR)
-            spread_in = depth_pos[:, b, first : first + PAIR].unsqueeze(2).to_broadcast([P, PAIR, PLACES])
+        def gather(b, first, depths):
+            columns = slice(first * PLACES, (first + depths) * PLACES)
+            depth_rows = ring.tile([P, depths * PLACES], F32, name="depth_rows")
+            spread_out = depth_rows[:].rearrange("p (i t) -> p i t", i=depths)
+            spread_in = depth_pos[:, b, first : first + depths].unsqueeze(2).to_broadcast([P, depths, PLACES])
             if b == 0 and first == 0:
                 nc.vector.tensor_copy(spread_out, spread_in)
             else:
                 nc.scalar.activation(spread_out, spread_in, COPY)
             nc.vector.tensor_tensor(
                 results[b][:, columns],
-                tables[b][:].indirect(offsets[:, first * (PLACES // 16) : (first + PAIR) * (PLACES // 16)]),
+                tables[b][:].indirect(offsets[:, first * (PLACES // 16) : (first + depths) * (PLACES // 16)]),
                 depth_rows[:],
                 ADD,
             )
-            store_queues[(b + first // PAIR) % 2].dma_start(out_blocks[b][:, columns], results[b][:, columns])
-            for k in range(first, min(first + PAIR, DEPTHS - 1)):
+            store_queues[(b + first) % 2].dma_start(out_blocks[b][:, columns], results[b][:, columns])
+            for k in range(first, min(first + depths, DEPTHS - 1)):
                 tokens = results[b][:, k * PLACES : (k + 1) * PLACES]
                 nc.tensor.matmul(partials[b][:], identity[:], tokens, start=False, stop=(k == DEPTHS - 2))
 
@@ -81,6 +81,10 @@ def tile_rqtransformer_kernel(tc, tok_emb, dp_pos, sp_pos, offs, out):
             blocks = range(group, group + TURNS)
             for first in range(0, DEPTHS, PAIR):
                 for b in blocks:
-                    gather_pair(b, first)
+                    if b == BLOCKS - 1 and first == DEPTHS - PAIR:
+                        gather(b, first, 1)
+                        gather(b, first + 1, 1)
+                    else:
+                        gather(b, first, PAIR)
             for b in blocks:
                 finish(b)

@@ -14,7 +14,7 @@ PLACES = 512
 ENTRIES = DEPTHS * PLACES
 PAIR = 2
 BLOCKS = FEATURES // P
-TURNS = 2
+GROUPS = ((0,), (1,), (2, 3))
 
 
 def tile_rqtransformer_kernel(tc, tok_emb, dp_pos, sp_pos, offs, out):
@@ -77,8 +77,7 @@ def tile_rqtransformer_kernel(tc, tok_emb, dp_pos, sp_pos, offs, out):
             nc.vector.tensor_tensor(total, partials[b][:], results[b][:, ENTRIES - PLACES : ENTRIES], ADD)
             nc.sync.dma_start(out_blocks[b][:, ENTRIES:], total)
 
-        for group in range(0, BLOCKS, TURNS):
-            blocks = range(group, group + TURNS)
+        for blocks in GROUPS:
             for first in range(0, DEPTHS, PAIR):
                 for b in blocks:
                     if b == BLOCKS - 1 and first == DEPTHS - PAIR:

@@ -32,7 +32,7 @@ def tile_rqtransformer_kernel(tc, tok_emb, dp_pos, sp_pos, offs, out):
         out_blocks = out.rearrange("(p b) j -> b p j", b=BLOCKS)
 
         depth_pos = held.tile([P, BLOCKS, DEPTHS], F32, name="depth_pos")
-        nc.scalar.dma_start(depth_pos[:], dp_pos.rearrange("(p b) k -> p b k", b=BLOCKS))
+        nc.sync.dma_start(depth_pos[:], dp_pos.rearrange("(p b) k -> p b k", b=BLOCKS))
 
         tables, place_pos = [], []
         for b in range(BLOCKS):

@@ -57,10 +57,7 @@ def tile_rqtransformer_kernel(tc, tok_emb, dp_pos, sp_pos, offs, out):
             depth_rows = ring.tile([P, depths * PLACES], F32, name="depth_rows")
             spread_out = depth_rows[:].rearrange("p (i t) -> p i t", i=depths)
             spread_in = depth_pos[:, b, first : first + depths].unsqueeze(2).to_broadcast([P, depths, PLACES])
-            if b == 0 and first == 0:
-                nc.vector.tensor_copy(spread_out, spread_in)
-            else:
-                nc.scalar.activation(spread_out, spread_in, COPY)
+            nc.scalar.activation(spread_out, spread_in, COPY)
             nc.vector.tensor_tensor(
                 results[b][:, columns],
                 tables[b][:].indirect(offsets[:, first * (PLACES // 16) : (first + depths) * (PLACES // 16)]),

@@ -14,14 +14,17 @@ PLACES = 512
 ENTRIES = DEPTHS * PLACES
 PAIR = 2
 BLOCKS = FEATURES // P
-GROUPS = ((0,), (1,), (2, 3))
+SQUARES = PLACES // P
+TURNED = (2, 3)
+UPRIGHT = (0, 1)
+GATHERS = 10
 
 
 def tile_rqtransformer_kernel(tc, tok_emb, dp_pos, sp_pos, offs, out):
     nc = tc.nc
     with (
         tc.tile_pool(name="held", bufs=1) as held,
-        tc.tile_pool(name="ring", bufs=4) as ring,
+        tc.tile_pool(name="rows", bufs=GATHERS) as rows,
         tc.psum_pool(name="banks", bufs=1) as banks,
     ):
         offsets = held.tile([P, ENTRIES // 16], U16, name="offsets")
@@ -34,27 +37,52 @@ def tile_rqtransformer_kernel(tc, tok_emb, dp_pos, sp_pos, offs, out):
         depth_pos = held.tile([P, BLOCKS, DEPTHS], F32, name="depth_pos")
         nc.sync.dma_start(depth_pos[:], dp_pos.rearrange("(p b) k -> p b k", b=BLOCKS))
 
-        tables, place_pos = [], []
+        tables, place_pos, results = [], [], []
         for b in range(BLOCKS):
             tables.append(held.tile([P, CODES], F32, name=f"table{b}"))
             nc.sync.dma_start(tables[b][:], table_blocks[b])
             place_pos.append(held.tile([P, PLACES], F32, name=f"place_pos{b}"))
             nc.sync.dma_start(place_pos[b][:], place_blocks[b])
+            results.append(held.tile([P, ENTRIES + PLACES], F32, name=f"result{b}"))
 
         identity = held.tile([P, P], F32, name="identity")
         make_identity(nc, identity[:])
 
-        store_queues = (nc.sync, nc.scalar)
+        def tokens(b, k):
+            return results[b][:, k * PLACES : (k + 1) * PLACES]
 
-        results, partials = [], []
+        def add_upright(bank, term, first, last):
+            nc.tensor.matmul(bank[:], identity[:], term, start=first, stop=last)
+
+        def add_turned(bank, term, first, last):
+            for s in range(SQUARES):
+                square = slice(s * P, (s + 1) * P)
+                nc.tensor.matmul(
+                    bank[:, square], lhsT=term[:, square], rhs=identity[:], is_transpose=True,
+                    start=(first and s == 0), stop=(last and s == SQUARES - 1),
+                )
+
+        upright = [banks.tile([P, PLACES], F32, name=f"upright{b}") for b in range(BLOCKS)]
+        flipped = {b: banks.tile([P, PLACES], F32, name=f"flipped{b}") for b in TURNED}
+
         for b in range(BLOCKS):
-            results.append(held.tile([P, ENTRIES + PLACES], F32, name=f"result{b}"))
-            partials.append(banks.tile([P, PLACES], F32, name=f"partial{b}"))
-            nc.tensor.matmul(partials[b][:], identity[:], place_pos[b][:], start=True, stop=False)
+            if b in TURNED:
+                add_turned(flipped[b], place_pos[b][:], True, False)
+            else:
+                add_upright(upright[b], place_pos[b][:], True, False)
+
+        def add_tokens(b, k):
+            if b not in TURNED:
+                if k < DEPTHS - 1:
+                    add_upright(upright[b], tokens(b, k), False, k == DEPTHS - 2)
+            elif k % 2 == 0:
+                add_turned(flipped[b], tokens(b, k), False, k == DEPTHS - 2)
+            else:
+                add_upright(upright[b], tokens(b, k), k == 1, False)
 
         def gather(b, first, depths):
             columns = slice(first * PLACES, (first + depths) * PLACES)
-            depth_rows = ring.tile([P, depths * PLACES], F32, name="depth_rows")
+            depth_rows = rows.tile([P, depths * PLACES], F32, name="depth_rows")
             spread_out = depth_rows[:].rearrange("p (i t) -> p i t", i=depths)
             spread_in = depth_pos[:, b, first : first + depths].unsqueeze(2).to_broadcast([P, depths, PLACES])
             nc.scalar.activation(spread_out, spread_in, COPY)
@@ -64,23 +92,30 @@ def tile_rqtransformer_kernel(tc, tok_emb, dp_pos, sp_pos, offs, out):
                 depth_rows[:],
                 ADD,
             )
-            store_queues[(b + first) % 2].dma_start(out_blocks[b][:, columns], results[b][:, columns])
-            for k in range(first, min(first + depths, DEPTHS - 1)):
-                tokens = results[b][:, k * PLACES : (k + 1) * PLACES]
-                nc.tensor.matmul(partials[b][:], identity[:], tokens, start=False, stop=(k == DEPTHS - 2))
+            nc.sync.dma_start(out_blocks[b][:, columns], results[b][:, columns])
+            for k in range(first, first + depths):
+                add_tokens(b, k)
 
         def finish(b):
             total = results[b][:, ENTRIES:]
-            nc.vector.tensor_tensor(total, partials[b][:], results[b][:, ENTRIES - PLACES : ENTRIES], ADD)
-            nc.sync.dma_start(out_blocks[b][:, ENTRIES:], total)
+            if b in TURNED:
+                flipped_part = held.tile([P, PLACES], F32, name=f"flipped_part{b}")
+                nc.scalar.activation(flipped_part[:], flipped[b][:], COPY)
+                add_turned(upright[b], flipped_part[:], False, True)
+                nc.scalar.activation(total, upright[b][:], COPY)
+                nc.scalar.dma_start(out_blocks[b][:, ENTRIES:], total)
+            else:
+                nc.vector.tensor_tensor(total, upright[b][:], tokens(b, DEPTHS - 1), ADD)
+                nc.sync.dma_start(out_blocks[b][:, ENTRIES:], total)
 
-        for blocks in GROUPS:
-            for first in range(0, DEPTHS, PAIR):
-                for b in blocks:
-                    if b == BLOCKS - 1 and first == DEPTHS - PAIR:
-                        gather(b, first, 1)
-                        gather(b, first + 1, 1)
-                    else:
-                        gather(b, first, PAIR)
-            for b in blocks:
-                finish(b)
+        for b in UPRIGHT:
+            gather(b, 0, PAIR)
+        for b in TURNED:
+            gather(b, 0, PAIR)
+            gather(b, PAIR, PAIR)
+            finish(b)
+        for k in range(PAIR, DEPTHS):
+            for b in UPRIGHT:
+                gather(b, k, 1)
+        for b in UPRIGHT:
+            finish(b)

@@ -17,7 +17,7 @@ BLOCKS = FEATURES // P
 SQUARES = PLACES // P
 TURNED = (2, 3)
 UPRIGHT = (0, 1)
-GATHERS = 10
+GATHERS = 9
 
 
 def tile_rqtransformer_kernel(tc, tok_emb, dp_pos, sp_pos, offs, out):
@@ -114,8 +114,8 @@ def tile_rqtransformer_kernel(tc, tok_emb, dp_pos, sp_pos, offs, out):
             gather(b, 0, PAIR)
             gather(b, PAIR, PAIR)
             finish(b)
-        for k in range(PAIR, DEPTHS):
-            for b in UPRIGHT:
-                gather(b, k, 1)
-        for b in UPRIGHT:
-            finish(b)
+        gather(UPRIGHT[1], PAIR, 1)
+        gather(UPRIGHT[0], PAIR, PAIR)
+        gather(UPRIGHT[1], PAIR + 1, 1)
+        finish(UPRIGHT[1])
+        finish(UPRIGHT[0])

@@ -114,8 +114,8 @@ def tile_rqtransformer_kernel(tc, tok_emb, dp_pos, sp_pos, offs, out):
             gather(b, 0, PAIR)
             gather(b, PAIR, PAIR)
             finish(b)
-        gather(UPRIGHT[1], PAIR, 1)
         gather(UPRIGHT[0], PAIR, PAIR)
+        gather(UPRIGHT[1], PAIR, 1)
         gather(UPRIGHT[1], PAIR + 1, 1)
-        finish(UPRIGHT[1])
-        finish(UPRIGHT[0])
+        for b in UPRIGHT:
+            finish(b)

import concourse.mybir as mybir
from concourse.masks import make_identity

F32 = mybir.dt.float32
U16 = mybir.dt.uint16
ADD = mybir.AluOpType.add
COPY = mybir.ActivationFunctionType.Copy

P = 128
FEATURES = 512
CODES = 1024
DEPTHS = 4
PLACES = 512
ENTRIES = DEPTHS * PLACES
PAIR = 2
BLOCKS = FEATURES // P
SQUARES = PLACES // P
TURNED = (2, 3)
UPRIGHT = (0, 1)
GATHERS = 9


def tile_rqtransformer_kernel(tc, tok_emb, dp_pos, sp_pos, offs, out):
    nc = tc.nc
    with (
        tc.tile_pool(name="held", bufs=1) as held,
        tc.tile_pool(name="rows", bufs=GATHERS) as rows,
        tc.psum_pool(name="banks", bufs=1) as banks,
    ):
        offsets = held.tile([P, ENTRIES // 16], U16, name="offsets")
        nc.sync.dma_start(offsets[:], offs)

        table_blocks = tok_emb.rearrange("(p b) v -> b p v", b=BLOCKS)
        place_blocks = sp_pos.rearrange("(p b) t -> b p t", b=BLOCKS)
        out_blocks = out.rearrange("(p b) j -> b p j", b=BLOCKS)

        depth_pos = held.tile([P, BLOCKS, DEPTHS], F32, name="depth_pos")
        nc.sync.dma_start(depth_pos[:], dp_pos.rearrange("(p b) k -> p b k", b=BLOCKS))

        tables, place_pos, results = [], [], []
        for b in range(BLOCKS):
            tables.append(held.tile([P, CODES], F32, name=f"table{b}"))
            nc.sync.dma_start(tables[b][:], table_blocks[b])
            place_pos.append(held.tile([P, PLACES], F32, name=f"place_pos{b}"))
            nc.sync.dma_start(place_pos[b][:], place_blocks[b])
            results.append(held.tile([P, ENTRIES + PLACES], F32, name=f"result{b}"))

        identity = held.tile([P, P], F32, name="identity")
        make_identity(nc, identity[:])

        def tokens(b, k):
            return results[b][:, k * PLACES : (k + 1) * PLACES]

        def add_upright(bank, term, first, last):
            nc.tensor.matmul(bank[:], identity[:], term, start=first, stop=last)

        def add_turned(bank, term, first, last):
            for s in range(SQUARES):
                square = slice(s * P, (s + 1) * P)
                nc.tensor.matmul(
                    bank[:, square], lhsT=term[:, square], rhs=identity[:], is_transpose=True,
                    start=(first and s == 0), stop=(last and s == SQUARES - 1),
                )

        upright = [banks.tile([P, PLACES], F32, name=f"upright{b}") for b in range(BLOCKS)]
        flipped = {b: banks.tile([P, PLACES], F32, name=f"flipped{b}") for b in TURNED}

        for b in range(BLOCKS):
            if b in TURNED:
                add_turned(flipped[b], place_pos[b][:], True, False)
            else:
                add_upright(upright[b], place_pos[b][:], True, False)

        def add_tokens(b, k):
            if b not in TURNED:
                if k < DEPTHS - 1:
                    add_upright(upright[b], tokens(b, k), False, k == DEPTHS - 2)
            elif k % 2 == 0:
                add_turned(flipped[b], tokens(b, k), False, k == DEPTHS - 2)
            else:
                add_upright(upright[b], tokens(b, k), k == 1, False)

        def gather(b, first, depths):
            columns = slice(first * PLACES, (first + depths) * PLACES)
            depth_rows = rows.tile([P, depths * PLACES], F32, name="depth_rows")
            spread_out = depth_rows[:].rearrange("p (i t) -> p i t", i=depths)
            spread_in = depth_pos[:, b, first : first + depths].unsqueeze(2).to_broadcast([P, depths, PLACES])
            nc.scalar.activation(spread_out, spread_in, COPY)
            nc.vector.tensor_tensor(
                results[b][:, columns],
                tables[b][:].indirect(offsets[:, first * (PLACES // 16) : (first + depths) * (PLACES // 16)]),
                depth_rows[:],
                ADD,
            )
            nc.sync.dma_start(out_blocks[b][:, columns], results[b][:, columns])
            for k in range(first, first + depths):
                add_tokens(b, k)

        def finish(b):
            total = results[b][:, ENTRIES:]
            if b in TURNED:
                flipped_part = held.tile([P, PLACES], F32, name=f"flipped_part{b}")
                nc.scalar.activation(flipped_part[:], flipped[b][:], COPY)
                add_turned(upright[b], flipped_part[:], False, True)
                nc.scalar.activation(total, upright[b][:], COPY)
                nc.scalar.dma_start(out_blocks[b][:, ENTRIES:], total)
            else:
                nc.vector.tensor_tensor(total, upright[b][:], tokens(b, DEPTHS - 1), ADD)
                nc.sync.dma_start(out_blocks[b][:, ENTRIES:], total)

        for b in UPRIGHT:
            gather(b, 0, PAIR)
        for b in TURNED:
            gather(b, 0, PAIR)
            gather(b, PAIR, PAIR)
            finish(b)
        gather(UPRIGHT[0], PAIR, PAIR)
        gather(UPRIGHT[1], PAIR, 1)
        gather(UPRIGHT[1], PAIR + 1, 1)
        for b in UPRIGHT:
            finish(b)
